import numpy as np
import ml_dtypes


def mxq(x, axis, fmt="e4m3"):
    dtype, down = {"e4m3": (ml_dtypes.float8_e4m3fn, 7), "e5m2": (ml_dtypes.float8_e5m2, 14)}[fmt]
    v = np.moveaxis(np.asarray(x, np.float32).astype(ml_dtypes.bfloat16).astype(np.float64), axis, -1)
    blocks = v.reshape(v.shape[:-1] + (-1, 32))
    amax = np.abs(blocks).max(-1, keepdims=True)
    byte = np.maximum(np.where(amax > 0, np.frexp(amax)[1] - 1 + 127, 0) - down, 1)
    scale = np.exp2(byte - 127.0)
    codes = (blocks / scale).astype(np.float32).astype(dtype).astype(np.float64)
    return np.moveaxis((codes * scale).reshape(v.shape), -1, axis)


WIDE = False


def mx_kscale(k):
    if not WIDE:
        return np.ones(k)
    levels = np.array([18, -18])
    if k % 512:
        return np.exp2(np.random.permutation(np.resize(levels, k // 32))).repeat(32)
    a = np.empty((k // 512, 16))
    for p in range(k // 512):
        a[p, :8] = np.random.permutation(np.resize(levels, 8))
        for g in range(8):
            far = levels[np.abs(levels - a[p, g]) >= 10]
            a[p, g + 8] = far[np.random.randint(len(far))]
    return np.exp2(a.ravel()).repeat(32)


BF16 = ml_dtypes.bfloat16


def bf(x):
    return np.asarray(x, np.float32).astype(BF16)


def f64(x):
    return np.asarray(x).astype(np.float64)


B, N, D1, D2, NS = 128, 8, 1024, 256, 2
ND = D1
NP = N // NS
T = B * N


def rolled_concat(arrays, n, axis=-1):
    return np.concatenate(arrays[n:] + arrays[:n], axis=axis)


def pair_means(x2):
    rows = []
    for spin in range(NS):
        r = x2[:, spin * NP:(spin + 1) * NP]
        means = [np.mean(r[:, :, c * NP:(c + 1) * NP], axis=2) for c in range(NS)]
        rows.append(rolled_concat(means, spin))
    return np.concatenate(rows, axis=1)


def pre_activation(in_1e, in_2e, W_unmixed, b_unmixed, W_mixed, W_2e):
    x1, x2 = f64(in_1e), f64(in_2e)
    dense_unmixed = x1 @ f64(W_unmixed) + f64(b_unmixed)
    means = [np.mean(x1[:, c * NP:(c + 1) * NP], axis=1, keepdims=True) for c in range(NS)]
    all_spins = np.concatenate([rolled_concat(means, c) for c in range(NS)], axis=1)
    dense_mixed = np.repeat(all_spins @ f64(W_mixed), NP, axis=1)
    dense_2e = pair_means(x2) @ f64(W_2e)
    return dense_unmixed + dense_mixed + dense_2e


def setup_inputs():
    s = mx_kscale(T).reshape(B, N)
    u = mx_kscale(ND)
    in_1e = bf(np.random.standard_normal((B, N, D1)))
    x20 = bf(np.random.standard_normal((B, N, N, D2)))
    W_unmixed = bf(np.random.standard_normal((D1, ND)) * 0.6 / np.sqrt(D1))
    b_unmixed = bf(np.random.standard_normal(ND) * 0.3)
    W_mixed = bf(np.random.standard_normal((NS * D1, ND)) * 0.6 * np.sqrt(NP) / np.sqrt(NS * D1))
    w20 = bf(np.random.standard_normal((NS * D2, ND)) * 0.6 * np.sqrt(NP) / np.sqrt(NS * D2))
    z = pre_activation(in_1e, x20, W_unmixed, b_unmixed, W_mixed, w20)
    g = np.random.standard_normal((B, N, ND)) * np.exp2(np.random.randint(-6, 1, (B, N, 1))) * 4.0
    return {"in_1e": in_1e,
            "in_2e": bf(f64(x20) * s[:, :, None, None]),
            "W_unmixed": W_unmixed,
            "b_unmixed": b_unmixed,
            "W_mixed": W_mixed,
            "W_2e": bf(f64(w20) / u),
            "z": np.asarray(z, np.float32),
            "grad_out": bf(g / s[:, :, None] * u)}


def reference(in_1e, in_2e, W_unmixed, b_unmixed, W_mixed, W_2e, z, grad_out):
    th = np.tanh(f64(z))
    dz = (f64(grad_out) * (1.0 - th * th)).reshape(T, ND)
    all_2e = pair_means(f64(in_2e)).reshape(T, NS * D2)
    d_all = mxq(dz, 1, "e5m2") @ mxq(f64(W_2e), 1, "e4m3").T
    dw = mxq(all_2e, 0, "e4m3").T @ mxq(dz, 0, "e5m2")
    d_all = d_all.reshape(B, N, NS, D2) / NP
    dx = np.zeros((B, N, N, D2))
    for i in range(NS):
        for j in range(NS):
            block = d_all[:, i * NP:(i + 1) * NP, (j - i) % NS]
            dx[:, i * NP:(i + 1) * NP, j * NP:(j + 1) * NP] = block[:, :, None, :]
    return dx, dw

@@ -1,0 +1,355 @@
+from contextlib import ExitStack
+
+import concourse.mybir as mybir
+from concourse.masks import make_identity
+
+F32 = mybir.dt.float32
+BF16 = mybir.dt.bfloat16
+U32 = mybir.dt.uint32
+U8 = mybir.dt.uint8
+E4M3 = mybir.dt.float8_e4m3fn_x4
+E5M2 = mybir.dt.float8_e5m2_x4
+ACT = mybir.ActivationFunctionType
+ALU = mybir.AluOpType
+
+P = 128
+TOKENS, FEATS, PAIR, COLS = 1024, 1024, 256, 512
+FLOPS = 2 * 2 * TOKENS * FEATS * COLS
+BYTES = 2 * 8 * TOKENS * PAIR + 2 * COLS * FEATS + 6 * TOKENS * FEATS + 4 * 8 * TOKENS * PAIR + 4 * COLS * FEATS
+
+
+def tile_ferminetoneelectronlayer_pa_v_kernel(
+    tc, in_1e, in_2e, W_unmixed, b_unmixed, W_mixed, W_2e, z, grad_out, out_0, out_1
+):
+    nc = tc.nc
+    z_hbm = z.rearrange("b i f -> (b i) f").rearrange("(g p j) f -> j p g f", g=2, j=4)
+    g_hbm = grad_out.rearrange("b i f -> (b i) f").rearrange("(g p j) f -> j p g f", g=2, j=4)
+    w_hbm = W_2e.rearrange("(r p) f -> p r f", p=P)
+    x_hbm = in_2e.rearrange("b i j d -> (b i j) d").rearrange("(q m r) d -> q r m d", q=4, r=P)
+
+    with ExitStack() as ctx:
+        sb = ctx.enter_context(tc.tile_pool(name="sb", bufs=1))
+        ps = ctx.enter_context(tc.psum_pool(name="ps", bufs=1))
+        ctx.enter_context(tc.manual_schedule())
+
+        def keep(name, cols, dtype):
+            return sb.tile([P, cols], dtype, name=name, tag=name, align_bytes=64)
+
+        zt = [keep("z%d" % j, 2 * FEATS, F32) for j in range(4)]
+        gt = [keep("g%d" % j, 2 * FEATS, BF16) for j in range(4)]
+        wt = keep("w", 4 * FEATS, BF16)
+        xt = [keep("x%d" % q, 16 * PAIR, BF16) for q in range(4)]
+        ident = keep("ident", P, F32)
+        pick = keep("pick", 32, BF16)
+        dz = keep("dz", 8 * FEATS, BF16)
+        w_grp = [keep("w_grp%d" % h, 2048, BF16) for h in range(2)]
+        w_code = [keep("w_code%d" % h, 512, U32) for h in range(2)]
+        w_scale = [keep("w_scale%d" % h, 512, U8) for h in range(2)]
+        mean_t = [keep("mean_t%d" % g, 2048, BF16) for g in range(2)]
+        mean_grp = [keep("mean_grp%d" % g, 2048, BF16) for g in range(2)]
+        mean_code = [keep("mean_code%d" % g, 512, U32) for g in range(2)]
+        mean_scale = [keep("mean_scale%d" % g, 512, U8) for g in range(2)]
+        tok_code = [[keep("tok_code%d%d" % (g, h), 512, U32) for h in range(2)] for g in range(2)]
+        tok_scale = [[keep("tok_scale%d%d" % (g, h), 512, U8) for h in range(2)] for g in range(2)]
+        d_all = [keep("d_all%d" % i, COLS, F32) for i in range(8)]
+        dw = [keep("dw%d" % m, FEATS, F32) for m in range(4)]
+
+        def load_z(j, g0, g1):
+            nc.sync.dma_start(
+                out=zt[j][:, g0 * FEATS : g1 * FEATS].rearrange("p (g f) -> p g f", f=FEATS), in_=z_hbm[j, :, g0:g1, :]
+            )
+
+        def load_g(j):
+            nc.sync.dma_start(out=gt[j][:].rearrange("p (g f) -> p g f", g=2), in_=g_hbm[j])
+
+        nc.sync.dma_start(out=wt[:].rearrange("p (r f) -> p r f", r=4), in_=w_hbm)
+        load_z(0, 0, 1)
+        load_g(0)
+        load_z(0, 1, 2)
+        for j in range(1, 4):
+            load_z(j, 0, 2)
+            load_g(j)
+        for q in range(4):
+            nc.sync.dma_start(out=xt[q][:].rearrange("r (m d) -> r m d", m=16), in_=x_hbm[q])
+
+        make_identity(nc, ident[:])
+        nc.gpsimd.memset(pick[:], -0.25)
+        for half in range(2):
+            cols = pick[:, 16 * half : 16 * half + 16]
+            steps = (16, 64, 36 - 8 * half, 8)
+            nc.gpsimd.affine_select(
+                out=cols, in_=cols, pattern=[[-s, 2] for s in steps], compare_op=ALU.is_ge, fill=0.0,
+                base=-4 * half, channel_multiplier=1,
+            )
+            nc.gpsimd.affine_select(
+                out=cols, in_=cols, pattern=[[s, 2] for s in steps], compare_op=ALU.is_ge, fill=0.0,
+                base=4 * half + 3, channel_multiplier=-1,
+            )
+
+        def bank_tile(n):
+            return ps.tile([P, 512], F32, name="bank%d" % n, tag="bank%d" % n)
+
+        def quantize(code, scale, src, fmt):
+            nc.vector.quantize_mx(out=code.bitcast(fmt), scales=scale, in_=src)
+
+        def tanh_squared(j, g0, g1):
+            part = zt[j][:, g0 * FEATS : g1 * FEATS]
+            nc.scalar.activation(out=part, in_=part, func=ACT.Tanh)
+            nc.scalar.activation(out=part, in_=part, func=ACT.Square)
+
+        def w_turn(h, rp):
+            words = wt[:].bitcast(F32)
+            bank = bank_tile(2 * h + rp)
+            for r in range(2):
+                for u in range(2):
+                    first = (2 * rp + r) * 512 + h * 256
+                    nc.tensor.transpose(
+                        bank[:, (2 * r + u) * P : (2 * r + u + 1) * P], words[:, first + u : first + 256 : 2], ident[:]
+                    )
+            nc.vector.tensor_copy(
+                out=w_grp[h][:].bitcast(F32)[:, rp * 512 : (rp + 1) * 512].rearrange("q (r p u) -> q r p u", r=2, u=2),
+                in_=bank[:].rearrange("q (r u p) -> q r p u", r=2, u=2),
+            )
+
+        def w_quantize(h):
+            quantize(w_code[h][:], w_scale[h][:], w_grp[h][:], E4M3)
+
+        def move(engine, out, in_):
+            if engine == "scalar":
+                nc.scalar.copy(out=out, in_=in_)
+            else:
+                nc.vector.tensor_copy(out=out, in_=in_)
+
+        def make_dz(j, u, g0=0, g1=2):
+            first = (2 * j + u) * FEATS
+            part = slice(g0 * FEATS, g1 * FEATS)
+            nc.vector.scalar_tensor_tensor(
+                out=dz[:, first + g0 * 512 : first + g1 * 512].rearrange("p (n e) -> p n e", e=2),
+                in0=zt[j][:, part].rearrange("p (n u e) -> p u n e", u=2, e=2)[:, u],
+                scalar=1.0,
+                in1=gt[j][:, part].rearrange("p (n u e) -> p u n e", u=2, e=2)[:, u],
+                op0=ALU.subtract,
+                op1=ALU.mult,
+            )
+
+        feat = {}
+
+        f_banks = {}
+
+        def dz_turn(j):
+            words = dz[:].bitcast(F32)
+            banks = [bank_tile(0), bank_tile(1)]
+            for u in range(2):
+                for h in range(2):
+                    for g in range(2):
+                        first = j * 1024 + u * 512 + g * 256 + h * P
+                        nc.tensor.transpose(
+                            banks[h][:, (2 * g + u) * P : (2 * g + u + 1) * P], words[:, first : first + P], ident[:]
+                        )
+            f_banks[j] = banks
+
+        def feat_out(j, engine):
+            banks = f_banks[j]
+            grp = sb.tile([P, 2048], BF16, name="feat_grp", tag="feat_grp", bufs=2, align_bytes=64)
+            code = sb.tile([P, 512], U32, name="feat_code", tag="feat_code", bufs=2, align_bytes=64)
+            scale = sb.tile([P, 512], U8, name="feat_scale", tag="feat_scale", bufs=2, align_bytes=64)
+            for h in range(2):
+                move(
+                    engine,
+                    out=grp[:].bitcast(F32)[:, h * 512 : (h + 1) * 512].rearrange(
+                        "q (s g b u) -> q s g b u", s=2, g=2, u=2
+                    ),
+                    in_=banks[h][:].rearrange("q (g u b s) -> q s g b u", g=2, u=2, s=2),
+                )
+            feat[j] = (code, scale, grp)
+
+        def feat_quantize(j):
+            code, scale, grp = feat[j]
+            for h in range(2):
+                quantize(
+                    code[:, h * 256 : (h + 1) * 256], scale[:, h * 256 : (h + 1) * 256],
+                    grp[:, h * 1024 : (h + 1) * 1024], E5M2,
+                )
+
+        d_banks = {}
+
+        def d_all_matmul(j):
+            code, scale, grp = feat[j]
+            for s in range(2):
+                bank = bank_tile(2 + s)
+                for h in range(2):
+                    cols = slice((2 * h + s) * P, (2 * h + s + 1) * P)
+                    nc.tensor.matmul_mx(
+                        out=bank[:], lhsT=code[:, cols].bitcast(E5M2), lhsT_scale=scale[:, cols],
+                        rhs=w_code[h][:].bitcast(E4M3), rhs_scale=w_scale[h][:], start=(h == 0), stop=(h == 1),
+                    )
+                d_banks[(j, s)] = bank
+
+        def d_all_out(j, engine):
+            for s in range(2):
+                i = 4 * s + j
+                if engine == "scalar":
+                    nc.scalar.activation(out=d_all[i][:], in_=d_banks[(j, s)][:], func=ACT.Copy, scale=-0.25)
+                else:
+                    nc.vector.tensor_scalar(
+                        out=d_all[i][:], in0=d_banks[(j, s)][:], scalar1=-0.25, scalar2=None, op0=ALU.mult
+                    )
+                for half in range(2):
+                    c = s if half == 0 else 1 - s
+                    nc.sync.dma_start(
+                        out=out_0[:, i, 4 * c : 4 * c + 4, :],
+                        in_=d_all[i][:, half * PAIR : (half + 1) * PAIR].unsqueeze(1).to_broadcast([P, 4, PAIR]),
+                    )
+
+        s_banks = {}
+
+        def mean_matmul(q):
+            for dh in range(2):
+                bank = bank_tile(4 + 2 * (q % 2) + dh)
+                for m in range(16):
+                    first = m * PAIR + dh * P
+                    nc.tensor.matmul(
+                        out=bank[:, m * 32 : (m + 1) * 32], lhsT=xt[q][:, first : first + P], rhs=pick[:],
+                        start=True, stop=True,
+                    )
+                s_banks[(q, dh)] = bank
+
+        def mean_out(q):
+            g, hq = divmod(q, 2)
+            for dh in range(2):
+                nc.scalar.copy(
+                    out=mean_t[g][:, dh * 1024 : (dh + 1) * 1024].rearrange(
+                        "d (k a m x) -> d a k m x", k=4, a=2, m=16
+                    )[:, hq],
+                    in_=s_banks[(q, dh)][:].rearrange("d (m k x) -> d k m x", k=4, x=8),
+                )
+
+        m_banks = {}
+
+        def mean_turn(g, first_bank):
+            words = mean_t[g][:].bitcast(F32)
+            for half in range(2):
+                bank = bank_tile(first_bank + half)
+                for dh in range(2):
+                    for u in range(2):
+                        first = dh * 512 + (2 * half + u) * P
+                        nc.tensor.transpose(
+                            bank[:, (2 * dh + u) * P : (2 * dh + u + 1) * P], words[:, first : first + P], ident[:]
+                        )
+                m_banks[(g, half)] = bank
+
+        def mean_turn_out(g):
+            for half in range(2):
+                bank = m_banks[(g, half)]
+                nc.scalar.copy(
+                    out=mean_grp[g][:].bitcast(F32)[:, half * 512 : (half + 1) * 512].rearrange(
+                        "p (a d u) -> p a d u", a=2, u=2
+                    ),
+                    in_=bank[:].rearrange("p (a u d) -> p a d u", a=2, u=2),
+                )
+
+        def mean_quantize(g):
+            quantize(mean_code[g][:], mean_scale[g][:], mean_grp[g][:], E4M3)
+
+        tok_grp = {}
+
+        def tok_interleave(g, h):
+            grp = sb.tile([P, 2048], BF16, name="tok_grp", tag="tok_grp", bufs=2, align_bytes=64)
+            nc.vector.tensor_copy(
+                out=grp[:].rearrange("p (u c i t) -> p u c t i", u=2, i=4, t=4),
+                in_=dz[:].rearrange("p (t u g h c i) -> p g h u c t i", t=4, u=2, g=2, h=2, i=4)[:, g, h],
+            )
+            tok_grp[(g, h)] = grp
+
+        def tok_quantize(g, h):
+            quantize(tok_code[g][h][:], tok_scale[g][h][:], tok_grp[(g, h)][:], E5M2)
+
+        w_banks = {}
+
+        def dw_pass(m, h, g):
+            if g == 0:
+                w_banks[(m, h)] = bank_tile(2 * m + h)
+            cols = slice(m * P, (m + 1) * P)
+            nc.tensor.matmul_mx(
+                out=w_banks[(m, h)][:], lhsT=mean_code[g][:, cols].bitcast(E4M3), lhsT_scale=mean_scale[g][:, cols],
+                rhs=tok_code[g][h][:].bitcast(E5M2), rhs_scale=tok_scale[g][h][:], start=(g == 0), stop=(g == 1),
+            )
+
+        def dw_out(m, h, engine):
+            move(
+                engine,
+                out=dw[m][:, h * 512 : (h + 1) * 512].rearrange("m (w u e) -> m w u e", u=2, e=2),
+                in_=w_banks[(m, h)][:].rearrange("m (u w e) -> m w u e", u=2, e=2),
+            )
+
+        tanh_squared(0, 0, 1)
+        w_turn(0, 0)
+        w_turn(0, 1)
+        w_turn(1, 0)
+        w_quantize(0)
+        w_turn(1, 1)
+        tanh_squared(0, 1, 2)
+        make_dz(0, 0, 0, 1)
+        make_dz(0, 1, 0, 1)
+        w_quantize(1)
+        make_dz(0, 0, 1, 2)
+        make_dz(0, 1, 1, 2)
+        tanh_squared(1, 0, 2)
+        dz_turn(0)
+        feat_out(0, "vector")
+        feat_quantize(0)
+        d_all_matmul(0)
+        make_dz(1, 0)
+        make_dz(1, 1)
+        tanh_squared(2, 0, 2)
+        dz_turn(1)
+        d_all_out(0, "vector")
+        feat_out(1, "vector")
+        feat_quantize(1)
+        d_all_matmul(1)
+        make_dz(2, 0)
+        make_dz(2, 1)
+        tanh_squared(3, 0, 2)
+        dz_turn(2)
+        mean_matmul(0)
+        mean_matmul(1)
+        d_all_out(1, "vector")
+        feat_out(2, "vector")
+        feat_quantize(2)
+        d_all_matmul(2)
+        mean_out(0)
+        mean_out(1)
+        make_dz(3, 0)
+        make_dz(3, 1)
+        dz_turn(3)
+        mean_turn(0, 4)
+        mean_matmul(3)
+        d_all_out(2, "scalar")
+        feat_out(3, "scalar")
+        mean_turn_out(0)
+        mean_matmul(2)
+        tok_interleave(0, 0)
+        tok_interleave(0, 1)
+        feat_quantize(3)
+        d_all_matmul(3)
+        mean_out(3)
+        mean_out(2)
+        mean_turn(1, 6)
+        tok_quantize(0, 0)
+        tok_quantize(0, 1)
+        d_all_out(3, "scalar")
+        mean_turn_out(1)
+        tok_interleave(1, 0)
+        mean_quantize(0)
+        tok_interleave(1, 1)
+        for m in range(4):
+            for h in range(2):
+                dw_pass(m, h, 0)
+        tok_quantize(1, 0)
+        mean_quantize(1)
+        tok_quantize(1, 1)
+        for m in range(4):
+            for h in range(2):
+                dw_pass(m, h, 1)
+                dw_out(m, h, "scalar" if h == 0 else "vector")
+            nc.sync.dma_start(out=out_1[m * P : (m + 1) * P, :], in_=dw[m][:])

@@ -24,35 +24,34 @@ def tile_ferminetoneelectronlayer_pa_v_kernel(
     nc = tc.nc
     z_hbm = z.rearrange("b i f -> (b i) f").rearrange("(g p j) f -> j p g f", g=2, j=4)
     g_hbm = grad_out.rearrange("b i f -> (b i) f").rearrange("(g p j) f -> j p g f", g=2, j=4)
-    w_hbm = W_2e.rearrange("(r p) f -> p r f", p=P)
-    x_hbm = in_2e.rearrange("b i j d -> (b i j) d").rearrange("(q m r) d -> q r m d", q=4, r=P)
+    w_hbm = W_2e.rearrange("(p r) f -> p (r f)", p=P)
+    dx_hbm = out_0.rearrange("b i j d -> b (i j d)")
 
     with ExitStack() as ctx:
         sb = ctx.enter_context(tc.tile_pool(name="sb", bufs=1))
         ps = ctx.enter_context(tc.psum_pool(name="ps", bufs=1))
         ctx.enter_context(tc.manual_schedule())
 
-        def keep(name, cols, dtype):
-            return sb.tile([P, cols], dtype, name=name, tag=name, align_bytes=64)
+        def keep(name, cols, dtype, tag=None):
+            return sb.tile([P, cols], dtype, name=name, tag=tag or name, align_bytes=64)
 
         zt = [keep("z%d" % j, 2 * FEATS, F32) for j in range(4)]
         gt = [keep("g%d" % j, 2 * FEATS, BF16) for j in range(4)]
         wt = keep("w", 4 * FEATS, BF16)
-        xt = [keep("x%d" % q, 16 * PAIR, BF16) for q in range(4)]
+        xt = [keep("x%d" % g, 32 * PAIR, BF16) for g in range(2)]
         ident = keep("ident", P, F32)
-        pick = keep("pick", 32, BF16)
+        ident_bf = keep("ident_bf", P, BF16)
         dz = keep("dz", 8 * FEATS, BF16)
         w_grp = [keep("w_grp%d" % h, 2048, BF16) for h in range(2)]
         w_code = [keep("w_code%d" % h, 512, U32) for h in range(2)]
         w_scale = [keep("w_scale%d" % h, 512, U8) for h in range(2)]
-        mean_t = [keep("mean_t%d" % g, 2048, BF16) for g in range(2)]
         mean_grp = [keep("mean_grp%d" % g, 2048, BF16) for g in range(2)]
         mean_code = [keep("mean_code%d" % g, 512, U32) for g in range(2)]
         mean_scale = [keep("mean_scale%d" % g, 512, U8) for g in range(2)]
         tok_code = [[keep("tok_code%d%d" % (g, h), 512, U32) for h in range(2)] for g in range(2)]
         tok_scale = [[keep("tok_scale%d%d" % (g, h), 512, U8) for h in range(2)] for g in range(2)]
-        d_all = [keep("d_all%d" % i, COLS, F32) for i in range(8)]
-        dw = [keep("dw%d" % m, FEATS, F32) for m in range(4)]
+        stage = keep("stage", 8 * 1024, F32)
+        sums = [keep("sums%d" % g, 2048, BF16) for g in range(2)]
 
         def load_z(j, g0, g1):
             nc.sync.dma_start(
@@ -62,29 +61,34 @@ def tile_ferminetoneelectronlayer_pa_v_kernel(
         def load_g(j):
             nc.sync.dma_start(out=gt[j][:].rearrange("p (g f) -> p g f", g=2), in_=g_hbm[j])
 
-        nc.sync.dma_start(out=wt[:].rearrange("p (r f) -> p r f", r=4), in_=w_hbm)
+        def load_x(g):
+            walkers = in_2e[64 * g : 64 * g + 64]
+            nc.sync.dma_start(out=xt[g][0:P:2, :], in_=walkers[:, 0:4].rearrange("b i j d -> b (i j d)"))
+            for half in range(2):
+                c = 1 - half
+                nc.sync.dma_start(
+                    out=xt[g][1:P:2, :].rearrange("p (i a x) -> p a i x", i=4, a=2)[:, half],
+                    in_=walkers[:, 4:8, 4 * c : 4 * c + 4].rearrange("b i j d -> b i (j d)"),
+                )
+
+        def load_w(rp):
+            nc.sync.dma_start(out=wt[:, rp * 2048 : (rp + 1) * 2048], in_=w_hbm[:, rp * 2048 : (rp + 1) * 2048])
+
+        load_w(0)
         load_z(0, 0, 1)
-        load_g(0)
         load_z(0, 1, 2)
-        for j in range(1, 4):
-            load_z(j, 0, 2)
+        load_g(0)
+        load_z(1, 0, 2)
+        load_w(1)
+        for j in range(1, 3):
             load_g(j)
-        for q in range(4):
-            nc.sync.dma_start(out=xt[q][:].rearrange("r (m d) -> r m d", m=16), in_=x_hbm[q])
+            load_z(j + 1, 0, 2)
+        load_g(3)
+        load_x(0)
+        load_x(1)
 
         make_identity(nc, ident[:])
-        nc.gpsimd.memset(pick[:], -0.25)
-        for half in range(2):
-            cols = pick[:, 16 * half : 16 * half + 16]
-            steps = (16, 64, 36 - 8 * half, 8)
-            nc.gpsimd.affine_select(
-                out=cols, in_=cols, pattern=[[-s, 2] for s in steps], compare_op=ALU.is_ge, fill=0.0,
-                base=-4 * half, channel_multiplier=1,
-            )
-            nc.gpsimd.affine_select(
-                out=cols, in_=cols, pattern=[[s, 2] for s in steps], compare_op=ALU.is_ge, fill=0.0,
-                base=4 * half + 3, channel_multiplier=-1,
-            )
+        make_identity(nc, ident_bf[:])
 
         def bank_tile(n):
             return ps.tile([P, 512], F32, name="bank%d" % n, tag="bank%d" % n)
@@ -99,7 +103,7 @@ def tile_ferminetoneelectronlayer_pa_v_kernel(
 
         def w_turn(h, rp):
             words = wt[:].bitcast(F32)
-            bank = bank_tile(2 * h + rp)
+            bank = bank_tile(4 + 2 * rp + h)
             for r in range(2):
                 for u in range(2):
                     first = (2 * rp + r) * 512 + h * 256
@@ -107,8 +111,8 @@ def tile_ferminetoneelectronlayer_pa_v_kernel(
                         bank[:, (2 * r + u) * P : (2 * r + u + 1) * P], words[:, first + u : first + 256 : 2], ident[:]
                     )
             nc.vector.tensor_copy(
-                out=w_grp[h][:].bitcast(F32)[:, rp * 512 : (rp + 1) * 512].rearrange("q (r p u) -> q r p u", r=2, u=2),
-                in_=bank[:].rearrange("q (r u p) -> q r p u", r=2, u=2),
+                out=w_grp[h][:].bitcast(F32).rearrange("q (p a r u) -> q a p r u", a=2, r=2, u=2)[:, rp],
+                in_=bank[:].rearrange("q (r u p) -> q p r u", r=2, u=2),
             )
 
         def w_quantize(h):
@@ -176,7 +180,7 @@ def tile_ferminetoneelectronlayer_pa_v_kernel(
         def d_all_matmul(j):
             code, scale, grp = feat[j]
             for s in range(2):
-                bank = bank_tile(2 + s)
+                bank = bank_tile(2 + 2 * (j % 2) + s)
                 for h in range(2):
                     cols = slice((2 * h + s) * P, (2 * h + s + 1) * P)
                     nc.tensor.matmul_mx(
@@ -185,77 +189,93 @@ def tile_ferminetoneelectronlayer_pa_v_kernel(
                     )
                 d_banks[(j, s)] = bank
 
-        def d_all_out(j, engine):
+        def scaled_out(engine, out, in_):
+            if engine == "scalar":
+                nc.scalar.activation(out=out, in_=in_, func=ACT.Copy, scale=-0.25)
+            else:
+                nc.vector.tensor_scalar(out=out, in0=in_, scalar1=-0.25, scalar2=None, op0=ALU.mult)
+
+        def d_all_out(j, engine, reps):
             for s in range(2):
                 i = 4 * s + j
-                if engine == "scalar":
-                    nc.scalar.activation(out=d_all[i][:], in_=d_banks[(j, s)][:], func=ACT.Copy, scale=-0.25)
+                dst = stage[:, i * 1024 : (i + 1) * 1024].rearrange("b (c r d) -> b c r d", c=2, r=2)
+                src = d_banks[(j, s)][:].rearrange("b (a d) -> b a d", a=2)
+                if s == 0:
+                    scaled_out(engine, dst[:, :, 0:reps], src.unsqueeze(2).to_broadcast([P, 2, reps, PAIR]))
                 else:
-                    nc.vector.tensor_scalar(
-                        out=d_all[i][:], in0=d_banks[(j, s)][:], scalar1=-0.25, scalar2=None, op0=ALU.mult
-                    )
-                for half in range(2):
-                    c = s if half == 0 else 1 - s
-                    nc.sync.dma_start(
-                        out=out_0[:, i, 4 * c : 4 * c + 4, :],
-                        in_=d_all[i][:, half * PAIR : (half + 1) * PAIR].unsqueeze(1).to_broadcast([P, 4, PAIR]),
-                    )
+                    for c in range(2):
+                        scaled_out(
+                            engine, dst[:, c, 0:reps], src[:, 1 - c].unsqueeze(1).to_broadcast([P, reps, PAIR])
+                        )
+
+        def d_all_repeat(j):
+            both = stage[:].rearrange("b (s j c r d) -> b j r s c d", s=2, j=4, c=2, r=2)[:, j]
+            nc.vector.tensor_copy(out=both[:, 1], in_=both[:, 0])
+
+        def dx_store(first, last, shift):
+            src = stage[:, shift : shift + 7 * 1024 + (1024 if shift == 0 else 0)].rearrange("b (i x) -> b i x", x=1024)
+            dst = dx_hbm[:, 2 * shift : 2 * shift + (8 if shift == 0 else 7) * 2048].rearrange("b (i x) -> b i x", x=2048)
+            step = max(last - first, 1)
+            nc.sync.dma_start(out=dst[:, first : last + 1 : step, 512:1536], in_=src[:, first : last + 1 : step])
+
+        def dx_stores(j):
+            if j == 0:
+                nc.sync.dma_start(out=dx_hbm[:, 0:512], in_=stage[:, 0:512])
+            dx_store(j, 4 + j, 0)
+            if j > 0:
+                dx_store(j - 1, 3 + j, 512)
+            if j == 3:
+                dx_store(3, 3, 512)
+                nc.sync.dma_start(out=dx_hbm[:, 16384 - 512 :], in_=stage[:, 8192 - 512 :])
 
         s_banks = {}
 
-        def mean_matmul(q):
-            for dh in range(2):
-                bank = bank_tile(4 + 2 * (q % 2) + dh)
-                for m in range(16):
-                    first = m * PAIR + dh * P
-                    nc.tensor.matmul(
-                        out=bank[:, m * 32 : (m + 1) * 32], lhsT=xt[q][:, first : first + P], rhs=pick[:],
-                        start=True, stop=True,
-                    )
-                s_banks[(q, dh)] = bank
-
-        def mean_out(q):
-            g, hq = divmod(q, 2)
-            for dh in range(2):
-                nc.scalar.copy(
-                    out=mean_t[g][:, dh * 1024 : (dh + 1) * 1024].rearrange(
-                        "d (k a m x) -> d a k m x", k=4, a=2, m=16
-                    )[:, hq],
-                    in_=s_banks[(q, dh)][:].rearrange("d (m k x) -> d k m x", k=4, x=8),
+        def sum_matmul(g, m, bank_no):
+            half, dh = divmod(m, 2)
+            bank = bank_tile(bank_no)
+            rows = xt[g][:].rearrange("p (i a j h d) -> p a h j i d", i=4, a=2, j=4, h=2)[:, half, dh]
+            for jj in range(4):
+                nc.tensor.matmul(
+                    out=bank[:].rearrange("p (i d) -> p i d", i=4), lhsT=ident_bf[:], rhs=rows[:, jj],
+                    start=(jj == 0), stop=(jj == 3),
                 )
+            s_banks[(g, m)] = bank
 
-        m_banks = {}
+        def sum_out(g, m):
+            nc.scalar.copy(
+                out=mean_grp[g][:, m * 512 : (m + 1) * 512].rearrange("p (d i) -> p d i", i=4),
+                in_=s_banks[(g, m)][:].rearrange("p (i d) -> p d i", i=4),
+            )
 
-        def mean_turn(g, first_bank):
-            words = mean_t[g][:].bitcast(F32)
-            for half in range(2):
-                bank = bank_tile(first_bank + half)
-                for dh in range(2):
-                    for u in range(2):
-                        first = dh * 512 + (2 * half + u) * P
-                        nc.tensor.transpose(
-                            bank[:, (2 * dh + u) * P : (2 * dh + u + 1) * P], words[:, first : first + P], ident[:]
-                        )
-                m_banks[(g, half)] = bank
+        pairs = {}
 
-        def mean_turn_out(g):
-            for half in range(2):
-                bank = m_banks[(g, half)]
-                nc.scalar.copy(
-                    out=mean_grp[g][:].bitcast(F32)[:, half * 512 : (half + 1) * 512].rearrange(
-                        "p (a d u) -> p a d u", a=2, u=2
-                    ),
-                    in_=bank[:].rearrange("p (a u d) -> p a d u", a=2, u=2),
-                )
+        def sum_pairs(g, half, width):
+            tmp = sb.tile([P, 2048], F32, name="pairs", tag="pairs", bufs=2, align_bytes=64)
+            rows = xt[g][:].rearrange("p (i a k j d) -> p a k i j d", i=4, a=2, k=2, j=2)[:, half]
+            view = tmp[:].rearrange("p (i j d) -> p i j d", i=4, j=2)[:, :, :, 0:width]
+            nc.vector.tensor_tensor(out=view, in0=rows[:, 0, :, :, 0:width], in1=rows[:, 1, :, :, 0:width], op=ALU.add)
+            pairs[(g, half)] = view
+
+        def sum_finish(g, half, width):
+            view = pairs[(g, half)]
+            dst = sums[g][:].rearrange("p (i a d) -> p a i d", i=4, a=2)[:, half, :, 0:width]
+            nc.vector.tensor_tensor(out=dst, in0=view[:, :, 0], in1=view[:, :, 1], op=ALU.add)
+
+        def sum_interleave(g, width):
+            nc.vector.tensor_copy(
+                out=mean_grp[g][:, 0 : 4 * width].rearrange("p (c i t) -> p c t i", i=4, t=4),
+                in_=sums[g][:].rearrange("p (t n) -> p t n", t=4)[:, :, 0:width].rearrange("p t (c i) -> p c t i", i=4),
+            )
 
         def mean_quantize(g):
             quantize(mean_code[g][:], mean_scale[g][:], mean_grp[g][:], E4M3)
 
         tok_grp = {}
 
-        def tok_interleave(g, h):
-            grp = sb.tile([P, 2048], BF16, name="tok_grp", tag="tok_grp", bufs=2, align_bytes=64)
-            nc.vector.tensor_copy(
+        def tok_interleave(g, h, engine):
+            grp = sb.tile([P, 2048], BF16, name="tok_grp", tag="tok_grp", bufs=4, align_bytes=64)
+            move(
+                engine,
                 out=grp[:].rearrange("p (u c i t) -> p u c t i", u=2, i=4, t=4),
                 in_=dz[:].rearrange("p (t u g h c i) -> p g h u c t i", t=4, u=2, g=2, h=2, i=4)[:, g, h],
             )
@@ -275,8 +295,12 @@ def tile_ferminetoneelectronlayer_pa_v_kernel(
                 rhs=tok_code[g][h][:].bitcast(E5M2), rhs_scale=tok_scale[g][h][:], start=(g == 0), stop=(g == 1),
             )
 
+        dw = {}
+
         def dw_out(m, h, engine):
-            move(
+            if h == 0:
+                dw[m] = keep("dw%d" % m, FEATS, F32, tag="z%d" % m)
+            scaled_out(
                 engine,
                 out=dw[m][:, h * 512 : (h + 1) * 512].rearrange("m (w u e) -> m w u e", u=2, e=2),
                 in_=w_banks[(m, h)][:].rearrange("m (u w e) -> m w u e", u=2, e=2),
@@ -284,72 +308,80 @@ def tile_ferminetoneelectronlayer_pa_v_kernel(
 
         tanh_squared(0, 0, 1)
         w_turn(0, 0)
-        w_turn(0, 1)
         w_turn(1, 0)
-        w_quantize(0)
-        w_turn(1, 1)
         tanh_squared(0, 1, 2)
         make_dz(0, 0, 0, 1)
         make_dz(0, 1, 0, 1)
-        w_quantize(1)
         make_dz(0, 0, 1, 2)
         make_dz(0, 1, 1, 2)
         tanh_squared(1, 0, 2)
         dz_turn(0)
         feat_out(0, "vector")
         feat_quantize(0)
-        d_all_matmul(0)
-        make_dz(1, 0)
-        make_dz(1, 1)
+        w_turn(0, 1)
+        w_turn(1, 1)
         tanh_squared(2, 0, 2)
+        make_dz(1, 0)
+        w_quantize(0)
+        make_dz(1, 1)
+        w_quantize(1)
         dz_turn(1)
-        d_all_out(0, "vector")
+        d_all_matmul(0)
         feat_out(1, "vector")
-        feat_quantize(1)
-        d_all_matmul(1)
-        make_dz(2, 0)
-        make_dz(2, 1)
         tanh_squared(3, 0, 2)
+        make_dz(2, 0)
+        feat_quantize(1)
+        make_dz(2, 1)
+        d_all_matmul(1)
         dz_turn(2)
-        mean_matmul(0)
-        mean_matmul(1)
-        d_all_out(1, "vector")
-        feat_out(2, "vector")
-        feat_quantize(2)
-        d_all_matmul(2)
-        mean_out(0)
-        mean_out(1)
+        d_all_out(0, "vector", 1)
+        feat_out(2, "scalar")
         make_dz(3, 0)
+        d_all_repeat(0)
+        dx_stores(0)
         make_dz(3, 1)
+        feat_quantize(2)
+        d_all_out(1, "scalar", 2)
+        dx_stores(1)
         dz_turn(3)
-        mean_turn(0, 4)
-        mean_matmul(3)
-        d_all_out(2, "scalar")
+        d_all_matmul(2)
         feat_out(3, "scalar")
-        mean_turn_out(0)
-        mean_matmul(2)
-        tok_interleave(0, 0)
-        tok_interleave(0, 1)
+        sum_pairs(0, 0, 256)
         feat_quantize(3)
         d_all_matmul(3)
-        mean_out(3)
-        mean_out(2)
-        mean_turn(1, 6)
+        for m in range(1, 4):
+            sum_matmul(1, m, (1, 7, 3)[m - 1])
+        tok_interleave(0, 0, "scalar")
+        d_all_out(2, "scalar", 2)
+        dx_stores(2)
+        d_all_out(3, "scalar", 2)
+        dx_stores(3)
+        sum_finish(0, 0, 256)
+        sum_pairs(0, 1, 256)
         tok_quantize(0, 0)
-        tok_quantize(0, 1)
-        d_all_out(3, "scalar")
-        mean_turn_out(1)
-        tok_interleave(1, 0)
+        sum_finish(0, 1, 256)
+        sum_pairs(1, 0, 128)
+        sum_interleave(0, 512)
+        sum_finish(1, 0, 128)
         mean_quantize(0)
-        tok_interleave(1, 1)
         for m in range(4):
-            for h in range(2):
-                dw_pass(m, h, 0)
+            dw_pass(m, 0, 0)
+        tok_interleave(1, 0, "scalar")
+        for m in range(1, 4):
+            sum_out(1, m)
+        tok_interleave(0, 1, "vector")
+        sum_interleave(1, 128)
+        tok_quantize(0, 1)
+        for m in range(4):
+            dw_pass(m, 1, 0)
+        tok_interleave(1, 1, "scalar")
         tok_quantize(1, 0)
         mean_quantize(1)
+        for m in range(4):
+            dw_pass(m, 0, 1)
+            dw_out(m, 0, "scalar")
         tok_quantize(1, 1)
         for m in range(4):
-            for h in range(2):
-                dw_pass(m, h, 1)
-                dw_out(m, h, "scalar" if h == 0 else "vector")
+            dw_pass(m, 1, 1)
+            dw_out(m, 1, "vector")
             nc.sync.dma_start(out=out_1[m * P : (m + 1) * P, :], in_=dw[m][:])

@@ -22,8 +22,9 @@ def tile_ferminetoneelectronlayer_pa_v_kernel(
     tc, in_1e, in_2e, W_unmixed, b_unmixed, W_mixed, W_2e, z, grad_out, out_0, out_1
 ):
     nc = tc.nc
-    z_hbm = z.rearrange("b i f -> (b i) f").rearrange("(g p j) f -> j p g f", g=2, j=4)
-    g_hbm = grad_out.rearrange("b i f -> (b i) f").rearrange("(g p j) f -> j p g f", g=2, j=4)
+    z_hbm = z.rearrange("b i f -> (b i) f").rearrange("(g p a j) f -> a g p (j f)", g=2, a=2, j=2)
+    g_hbm = grad_out.rearrange("b i f -> (b i) f").rearrange("(g p j) f -> g p (j f)", g=2, j=4)
+    x_hbm = in_2e[64:128].rearrange("b i j d -> (b i j) d").rearrange("(q m r l) d -> q r m (l d)", q=2, r=P, l=2)
     w_hbm = W_2e.rearrange("(p r) f -> p (r f)", p=P)
     dx_hbm = out_0.rearrange("b i j d -> b (i j d)")
 
@@ -36,9 +37,12 @@ def tile_ferminetoneelectronlayer_pa_v_kernel(
             return sb.tile([P, cols], dtype, name=name, tag=tag or name, align_bytes=64)
 
         zt = [keep("z%d" % j, 2 * FEATS, F32) for j in range(4)]
-        gt = [keep("g%d" % j, 2 * FEATS, BF16) for j in range(4)]
+        gt = [keep("g%d" % g, 4 * FEATS, BF16) for g in range(2)]
         wt = keep("w", 4 * FEATS, BF16)
-        xt = [keep("x%d" % g, 32 * PAIR, BF16) for g in range(2)]
+        xt = [keep("x0", 32 * PAIR, BF16)]
+        xq = [keep("xq%d" % q, 16 * PAIR, BF16) for q in range(2)]
+        pick = keep("pick", 64, BF16)
+        mean_t = keep("mean_t", 2048, BF16)
         ident = keep("ident", P, F32)
         ident_bf = keep("ident_bf", P, BF16)
         dz = keep("dz", 8 * FEATS, BF16)
@@ -51,15 +55,16 @@ def tile_ferminetoneelectronlayer_pa_v_kernel(
         tok_code = [[keep("tok_code%d%d" % (g, h), 512, U32) for h in range(2)] for g in range(2)]
         tok_scale = [[keep("tok_scale%d%d" % (g, h), 512, U8) for h in range(2)] for g in range(2)]
         stage = keep("stage", 8 * 1024, F32)
-        sums = [keep("sums%d" % g, 2048, BF16) for g in range(2)]
+        sums = [keep("sums0", 2048, BF16)]
 
-        def load_z(j, g0, g1):
-            nc.sync.dma_start(
-                out=zt[j][:, g0 * FEATS : g1 * FEATS].rearrange("p (g f) -> p g f", f=FEATS), in_=z_hbm[j, :, g0:g1, :]
-            )
+        def load_z(a, g, lo, hi):
+            nc.sync.dma_start(out=zt[2 * a + g][:, lo * FEATS : hi * FEATS], in_=z_hbm[a, g, :, lo * FEATS : hi * FEATS])
 
-        def load_g(j):
-            nc.sync.dma_start(out=gt[j][:].rearrange("p (g f) -> p g f", g=2), in_=g_hbm[j])
+        def load_g(g, lo, hi):
+            nc.sync.dma_start(out=gt[g][:, lo * FEATS : hi * FEATS], in_=g_hbm[g, :, lo * FEATS : hi * FEATS])
+
+        def load_xq(q):
+            nc.sync.dma_start(out=xq[q][:].rearrange("r (m x) -> r m x", m=8), in_=x_hbm[q])
 
         def load_x(g):
             walkers = in_2e[64 * g : 64 * g + 64]
@@ -74,21 +79,35 @@ def tile_ferminetoneelectronlayer_pa_v_kernel(
         def load_w(rp):
             nc.sync.dma_start(out=wt[:, rp * 2048 : (rp + 1) * 2048], in_=w_hbm[:, rp * 2048 : (rp + 1) * 2048])
 
+        load_z(0, 0, 0, 1)
         load_w(0)
-        load_z(0, 0, 1)
-        load_z(0, 1, 2)
-        load_g(0)
-        load_z(1, 0, 2)
+        load_z(0, 0, 1, 2)
+        load_z(0, 1, 0, 2)
+        load_g(0, 0, 2)
         load_w(1)
-        for j in range(1, 3):
-            load_g(j)
-            load_z(j + 1, 0, 2)
-        load_g(3)
+        load_z(1, 0, 0, 2)
+        load_g(1, 0, 2)
+        load_z(1, 1, 0, 2)
+        load_g(0, 2, 4)
+        load_g(1, 2, 4)
         load_x(0)
-        load_x(1)
+        load_xq(0)
+        load_xq(1)
 
         make_identity(nc, ident[:])
         make_identity(nc, ident_bf[:])
+        nc.gpsimd.memset(pick[:], 1.0)
+        for half in range(2):
+            cols = pick[:, 32 * half : 32 * half + 32]
+            dims = ((8, 2), (32, 4), (18 - 4 * half, 2), (4, 2))
+            nc.gpsimd.affine_select(
+                out=cols, in_=cols, pattern=[[-step, n] for step, n in dims], compare_op=ALU.is_ge, fill=0.0,
+                base=-2 * half, channel_multiplier=1,
+            )
+            nc.gpsimd.affine_select(
+                out=cols, in_=cols, pattern=[[step, n] for step, n in dims], compare_op=ALU.is_ge, fill=0.0,
+                base=2 * half + 1, channel_multiplier=-1,
+            )
 
         def bank_tile(n):
             return ps.tile([P, 512], F32, name="bank%d" % n, tag="bank%d" % n)
@@ -96,8 +115,8 @@ def tile_ferminetoneelectronlayer_pa_v_kernel(
         def quantize(code, scale, src, fmt):
             nc.vector.quantize_mx(out=code.bitcast(fmt), scales=scale, in_=src)
 
-        def tanh_squared(j, g0, g1):
-            part = zt[j][:, g0 * FEATS : g1 * FEATS]
+        def tanh_squared(a, g, lo=0, hi=2):
+            part = zt[2 * a + g][:, lo * FEATS : hi * FEATS]
             nc.scalar.activation(out=part, in_=part, func=ACT.Tanh)
             nc.scalar.activation(out=part, in_=part, func=ACT.Square)
 
@@ -124,14 +143,13 @@ def tile_ferminetoneelectronlayer_pa_v_kernel(
             else:
                 nc.vector.tensor_copy(out=out, in_=in_)
 
-        def make_dz(j, u, g0=0, g1=2):
-            first = (2 * j + u) * FEATS
-            part = slice(g0 * FEATS, g1 * FEATS)
+        def make_dz(a, g, u, lo=0, hi=2):
+            first = g * 4096 + u * 2048 + a * 1024
             nc.vector.scalar_tensor_tensor(
-                out=dz[:, first + g0 * 512 : first + g1 * 512].rearrange("p (n e) -> p n e", e=2),
-                in0=zt[j][:, part].rearrange("p (n u e) -> p u n e", u=2, e=2)[:, u],
+                out=dz[:, first + lo * 512 : first + hi * 512].rearrange("p (n e) -> p n e", e=2),
+                in0=zt[2 * a + g][:, lo * FEATS : hi * FEATS].rearrange("p (n u e) -> p u n e", u=2, e=2)[:, u],
                 scalar=1.0,
-                in1=gt[j][:, part].rearrange("p (n u e) -> p u n e", u=2, e=2)[:, u],
+                in1=gt[g][:, (2 * a + lo) * FEATS : (2 * a + hi) * FEATS].rearrange("p (n u e) -> p u n e", u=2, e=2)[:, u],
                 op0=ALU.subtract,
                 op1=ALU.mult,
             )
@@ -140,17 +158,16 @@ def tile_ferminetoneelectronlayer_pa_v_kernel(
 
         f_banks = {}
 
-        def dz_turn(j):
+        def dz_turn(j, g):
             words = dz[:].bitcast(F32)
-            banks = [bank_tile(0), bank_tile(1)]
+            if g == 0:
+                f_banks[j] = [bank_tile(2 * (j % 2) + h) for h in range(2)]
             for u in range(2):
                 for h in range(2):
-                    for g in range(2):
-                        first = j * 1024 + u * 512 + g * 256 + h * P
-                        nc.tensor.transpose(
-                            banks[h][:, (2 * g + u) * P : (2 * g + u + 1) * P], words[:, first : first + P], ident[:]
-                        )
-            f_banks[j] = banks
+                    first = g * 2048 + u * 1024 + j * 256 + h * P
+                    nc.tensor.transpose(
+                        f_banks[j][h][:, (2 * g + u) * P : (2 * g + u + 1) * P], words[:, first : first + P], ident[:]
+                    )
 
         def feat_out(j, engine):
             banks = f_banks[j]
@@ -177,10 +194,10 @@ def tile_ferminetoneelectronlayer_pa_v_kernel(
 
         d_banks = {}
 
-        def d_all_matmul(j):
+        def d_all_matmul(j, first_bank):
             code, scale, grp = feat[j]
             for s in range(2):
-                bank = bank_tile(2 + 2 * (j % 2) + s)
+                bank = bank_tile(first_bank + s)
                 for h in range(2):
                     cols = slice((2 * h + s) * P, (2 * h + s + 1) * P)
                     nc.tensor.matmul_mx(
@@ -267,6 +284,50 @@ def tile_ferminetoneelectronlayer_pa_v_kernel(
                 in_=sums[g][:].rearrange("p (t n) -> p t n", t=4)[:, :, 0:width].rearrange("p t (c i) -> p c t i", i=4),
             )
 
+        q_banks = {}
+
+        def pick_matmul(q, first_bank):
+            for dh in range(2):
+                bank = bank_tile(first_bank + dh)
+                for m in range(8):
+                    for jl in range(2):
+                        first = m * 512 + jl * PAIR + dh * P
+                        nc.tensor.matmul(
+                            out=bank[:, m * 64 : (m + 1) * 64], lhsT=xq[q][:, first : first + P], rhs=pick[:],
+                            start=(jl == 0), stop=(jl == 1),
+                        )
+                q_banks[(q, dh)] = bank
+
+        def pick_out(q):
+            for dh in range(2):
+                nc.scalar.copy(
+                    out=mean_t[:, dh * 1024 : (dh + 1) * 1024].rearrange("d (k a m x) -> d a k m x", k=4, a=2, m=8)[:, q],
+                    in_=q_banks[(q, dh)][:].rearrange("d (m k x) -> d k m x", k=4, x=16),
+                )
+
+        m_banks = {}
+
+        def mean_turn(first_bank):
+            words = mean_t[:].bitcast(F32)
+            for half in range(2):
+                bank = bank_tile(first_bank + half)
+                for dh in range(2):
+                    for u in range(2):
+                        first = dh * 512 + (2 * half + u) * P
+                        nc.tensor.transpose(
+                            bank[:, (2 * dh + u) * P : (2 * dh + u + 1) * P], words[:, first : first + P], ident[:]
+                        )
+                m_banks[half] = bank
+
+        def mean_turn_out():
+            for half in range(2):
+                nc.scalar.copy(
+                    out=mean_grp[1][:].bitcast(F32)[:, half * 512 : (half + 1) * 512].rearrange(
+                        "p (a d u) -> p a d u", a=2, u=2
+                    ),
+                    in_=m_banks[half][:].rearrange("p (a u d) -> p a d u", a=2, u=2),
+                )
+
         def mean_quantize(g):
             quantize(mean_code[g][:], mean_scale[g][:], mean_grp[g][:], E4M3)
 
@@ -277,7 +338,7 @@ def tile_ferminetoneelectronlayer_pa_v_kernel(
             move(
                 engine,
                 out=grp[:].rearrange("p (u c i t) -> p u c t i", u=2, i=4, t=4),
-                in_=dz[:].rearrange("p (t u g h c i) -> p g h u c t i", t=4, u=2, g=2, h=2, i=4)[:, g, h],
+                in_=dz[:].rearrange("p (g u t h c i) -> p g h u c t i", t=4, u=2, g=2, h=2, i=4)[:, g, h],
             )
             tok_grp[(g, h)] = grp
 
@@ -306,82 +367,84 @@ def tile_ferminetoneelectronlayer_pa_v_kernel(
                 in_=w_banks[(m, h)][:].rearrange("m (u w e) -> m w u e", u=2, e=2),
             )
 
-        tanh_squared(0, 0, 1)
+        tanh_squared(0, 0, 0, 1)
         w_turn(0, 0)
         w_turn(1, 0)
-        tanh_squared(0, 1, 2)
-        make_dz(0, 0, 0, 1)
-        make_dz(0, 1, 0, 1)
-        make_dz(0, 0, 1, 2)
-        make_dz(0, 1, 1, 2)
-        tanh_squared(1, 0, 2)
-        dz_turn(0)
-        feat_out(0, "vector")
-        feat_quantize(0)
+        tanh_squared(0, 0, 1, 2)
+        make_dz(0, 0, 0)
+        make_dz(0, 0, 1)
+        tanh_squared(0, 1)
         w_turn(0, 1)
         w_turn(1, 1)
-        tanh_squared(2, 0, 2)
-        make_dz(1, 0)
+        dz_turn(0, 0)
+        dz_turn(1, 0)
         w_quantize(0)
-        make_dz(1, 1)
+        tanh_squared(1, 0)
+        make_dz(0, 1, 0)
+        make_dz(0, 1, 1)
         w_quantize(1)
-        dz_turn(1)
-        d_all_matmul(0)
+        dz_turn(0, 1)
+        dz_turn(1, 1)
+        feat_out(0, "vector")
         feat_out(1, "vector")
-        tanh_squared(3, 0, 2)
-        make_dz(2, 0)
+        feat_quantize(0)
+        d_all_matmul(0, 4)
+        tanh_squared(1, 1)
+        make_dz(1, 0, 0)
         feat_quantize(1)
-        make_dz(2, 1)
-        d_all_matmul(1)
-        dz_turn(2)
-        d_all_out(0, "vector", 1)
-        feat_out(2, "scalar")
-        make_dz(3, 0)
-        d_all_repeat(0)
+        d_all_matmul(1, 6)
+        make_dz(1, 0, 1)
+        dz_turn(2, 0)
+        dz_turn(3, 0)
+        d_all_out(0, "scalar", 2)
         dx_stores(0)
-        make_dz(3, 1)
-        feat_quantize(2)
+        sum_matmul(0, 3, 4)
+        make_dz(1, 1, 0)
+        make_dz(1, 1, 1)
+        dz_turn(2, 1)
+        dz_turn(3, 1)
         d_all_out(1, "scalar", 2)
         dx_stores(1)
-        dz_turn(3)
-        d_all_matmul(2)
+        pick_matmul(0, 6)
+        feat_out(2, "scalar")
         feat_out(3, "scalar")
+        sum_out(0, 3)
         sum_pairs(0, 0, 256)
+        sum_pairs(0, 1, 128)
+        feat_quantize(2)
+        d_all_matmul(2, 0)
+        pick_matmul(1, 4)
+        sum_finish(0, 0, 256)
         feat_quantize(3)
-        d_all_matmul(3)
-        for m in range(1, 4):
-            sum_matmul(1, m, (1, 7, 3)[m - 1])
-        tok_interleave(0, 0, "scalar")
+        d_all_matmul(3, 2)
+        tok_interleave(0, 0, "vector")
+        pick_out(0)
         d_all_out(2, "scalar", 2)
         dx_stores(2)
+        pick_out(1)
+        mean_turn(6)
         d_all_out(3, "scalar", 2)
         dx_stores(3)
-        sum_finish(0, 0, 256)
-        sum_pairs(0, 1, 256)
+        mean_turn_out()
+        tok_interleave(1, 1, "scalar")
+        sum_finish(0, 1, 128)
         tok_quantize(0, 0)
-        sum_finish(0, 1, 256)
-        sum_pairs(1, 0, 128)
-        sum_interleave(0, 512)
-        sum_finish(1, 0, 128)
+        sum_interleave(0, 384)
+        tok_interleave(0, 1, "vector")
         mean_quantize(0)
         for m in range(4):
             dw_pass(m, 0, 0)
-        tok_interleave(1, 0, "scalar")
-        for m in range(1, 4):
-            sum_out(1, m)
-        tok_interleave(0, 1, "vector")
-        sum_interleave(1, 128)
+        tok_interleave(1, 0, "vector")
         tok_quantize(0, 1)
         for m in range(4):
             dw_pass(m, 1, 0)
-        tok_interleave(1, 1, "scalar")
-        tok_quantize(1, 0)
         mean_quantize(1)
+        tok_quantize(1, 0)
         for m in range(4):
             dw_pass(m, 0, 1)
-            dw_out(m, 0, "scalar")
         tok_quantize(1, 1)
         for m in range(4):
+            dw_out(m, 0, "scalar")
             dw_pass(m, 1, 1)
-            dw_out(m, 1, "vector")
+            dw_out(m, 1, "vector" if m < 3 else "scalar")
             nc.sync.dma_start(out=out_1[m * P : (m + 1) * P, :], in_=dw[m][:])

@@ -24,7 +24,6 @@ def tile_ferminetoneelectronlayer_pa_v_kernel(
     nc = tc.nc
     z_hbm = z.rearrange("b i f -> (b i) f").rearrange("(g p a j) f -> a g p (j f)", g=2, a=2, j=2)
     g_hbm = grad_out.rearrange("b i f -> (b i) f").rearrange("(g p j) f -> g p (j f)", g=2, j=4)
-    x_hbm = in_2e[64:128].rearrange("b i j d -> (b i j) d").rearrange("(q m r l) d -> q r m (l d)", q=2, r=P, l=2)
     w_hbm = W_2e.rearrange("(p r) f -> p (r f)", p=P)
     dx_hbm = out_0.rearrange("b i j d -> b (i j d)")
 
@@ -37,12 +36,11 @@ def tile_ferminetoneelectronlayer_pa_v_kernel(
             return sb.tile([P, cols], dtype, name=name, tag=tag or name, align_bytes=64)
 
         zt = [keep("z%d" % j, 2 * FEATS, F32) for j in range(4)]
-        gt = [keep("g%d" % g, 4 * FEATS, BF16) for g in range(2)]
+        g_early = [keep("g_early%d" % g, 2 * FEATS, BF16) for g in range(2)]
+        g_late = keep("g_late", 4 * FEATS, BF16)
+        gt = [g_early[0][:], g_early[1][:], g_late[:, 0 : 2 * FEATS], g_late[:, 2 * FEATS :]]
         wt = keep("w", 4 * FEATS, BF16)
-        xt = [keep("x0", 32 * PAIR, BF16)]
-        xq = [keep("xq%d" % q, 16 * PAIR, BF16) for q in range(2)]
-        pick = keep("pick", 64, BF16)
-        mean_t = keep("mean_t", 2048, BF16)
+        xt = [keep("x%d" % g, 32 * PAIR, BF16) for g in range(2)]
         ident = keep("ident", P, F32)
         ident_bf = keep("ident_bf", P, BF16)
         dz = keep("dz", 8 * FEATS, BF16)
@@ -55,7 +53,7 @@ def tile_ferminetoneelectronlayer_pa_v_kernel(
         tok_code = [[keep("tok_code%d%d" % (g, h), 512, U32) for h in range(2)] for g in range(2)]
         tok_scale = [[keep("tok_scale%d%d" % (g, h), 512, U8) for h in range(2)] for g in range(2)]
         stage = keep("stage", 8 * 1024, F32)
-        sums = [keep("sums0", 2048, BF16)]
+        sums = [keep("sums%d" % g, 2048, BF16) for g in range(2)]
 
         def load_z(a, g, lo, hi):
             nc.sync.dma_start(out=zt[2 * a + g][:, lo * FEATS : hi * FEATS], in_=z_hbm[a, g, :, lo * FEATS : hi * FEATS])
@@ -63,8 +61,11 @@ def tile_ferminetoneelectronlayer_pa_v_kernel(
         def load_g(g, lo, hi):
             nc.sync.dma_start(out=gt[g][:, lo * FEATS : hi * FEATS], in_=g_hbm[g, :, lo * FEATS : hi * FEATS])
 
-        def load_xq(q):
-            nc.sync.dma_start(out=xq[q][:].rearrange("r (m x) -> r m x", m=8), in_=x_hbm[q])
+        def load_g_late():
+            nc.sync.dma_start(
+                out=g_late[:].rearrange("p (g x) -> p g x", g=2),
+                in_=g_hbm.rearrange("g p x -> p g x")[:, :, 2 * FEATS :],
+            )
 
         def load_x(g):
             walkers = in_2e[64 * g : 64 * g + 64]
@@ -76,38 +77,24 @@ def tile_ferminetoneelectronlayer_pa_v_kernel(
                     in_=walkers[:, 4:8, 4 * c : 4 * c + 4].rearrange("b i j d -> b i (j d)"),
                 )
 
-        def load_w(rp):
-            nc.sync.dma_start(out=wt[:, rp * 2048 : (rp + 1) * 2048], in_=w_hbm[:, rp * 2048 : (rp + 1) * 2048])
+        def load_w(lo, hi):
+            nc.sync.dma_start(out=wt[:, lo * 2048 : hi * 2048], in_=w_hbm[:, lo * 2048 : hi * 2048])
 
         load_z(0, 0, 0, 1)
-        load_w(0)
+        load_w(0, 1)
         load_z(0, 0, 1, 2)
         load_z(0, 1, 0, 2)
         load_g(0, 0, 2)
-        load_w(1)
+        load_w(1, 2)
         load_z(1, 0, 0, 2)
         load_g(1, 0, 2)
         load_z(1, 1, 0, 2)
-        load_g(0, 2, 4)
-        load_g(1, 2, 4)
+        load_g_late()
         load_x(0)
-        load_xq(0)
-        load_xq(1)
+        load_x(1)
 
         make_identity(nc, ident[:])
         make_identity(nc, ident_bf[:])
-        nc.gpsimd.memset(pick[:], 1.0)
-        for half in range(2):
-            cols = pick[:, 32 * half : 32 * half + 32]
-            dims = ((8, 2), (32, 4), (18 - 4 * half, 2), (4, 2))
-            nc.gpsimd.affine_select(
-                out=cols, in_=cols, pattern=[[-step, n] for step, n in dims], compare_op=ALU.is_ge, fill=0.0,
-                base=-2 * half, channel_multiplier=1,
-            )
-            nc.gpsimd.affine_select(
-                out=cols, in_=cols, pattern=[[step, n] for step, n in dims], compare_op=ALU.is_ge, fill=0.0,
-                base=2 * half + 1, channel_multiplier=-1,
-            )
 
         def bank_tile(n):
             return ps.tile([P, 512], F32, name="bank%d" % n, tag="bank%d" % n)
@@ -115,10 +102,13 @@ def tile_ferminetoneelectronlayer_pa_v_kernel(
         def quantize(code, scale, src, fmt):
             nc.vector.quantize_mx(out=code.bitcast(fmt), scales=scale, in_=src)
 
-        def tanh_squared(a, g, lo=0, hi=2):
+        def tanh_squared(a, g, lo=0, hi=2, engine="scalar"):
             part = zt[2 * a + g][:, lo * FEATS : hi * FEATS]
             nc.scalar.activation(out=part, in_=part, func=ACT.Tanh)
-            nc.scalar.activation(out=part, in_=part, func=ACT.Square)
+            if engine == "scalar":
+                nc.scalar.activation(out=part, in_=part, func=ACT.Square)
+            else:
+                nc.vector.tensor_tensor(out=part, in0=part, in1=part, op=ALU.mult)
 
         def w_turn(h, rp):
             words = wt[:].bitcast(F32)
@@ -149,7 +139,7 @@ def tile_ferminetoneelectronlayer_pa_v_kernel(
                 out=dz[:, first + lo * 512 : first + hi * 512].rearrange("p (n e) -> p n e", e=2),
                 in0=zt[2 * a + g][:, lo * FEATS : hi * FEATS].rearrange("p (n u e) -> p u n e", u=2, e=2)[:, u],
                 scalar=1.0,
-                in1=gt[g][:, (2 * a + lo) * FEATS : (2 * a + hi) * FEATS].rearrange("p (n u e) -> p u n e", u=2, e=2)[:, u],
+                in1=gt[2 * a + g][:, lo * FEATS : hi * FEATS].rearrange("p (n u e) -> p u n e", u=2, e=2)[:, u],
                 op0=ALU.subtract,
                 op1=ALU.mult,
             )
@@ -284,63 +274,19 @@ def tile_ferminetoneelectronlayer_pa_v_kernel(
                 in_=sums[g][:].rearrange("p (t n) -> p t n", t=4)[:, :, 0:width].rearrange("p t (c i) -> p c t i", i=4),
             )
 
-        q_banks = {}
-
-        def pick_matmul(q, first_bank):
-            for dh in range(2):
-                bank = bank_tile(first_bank + dh)
-                for m in range(8):
-                    for jl in range(2):
-                        first = m * 512 + jl * PAIR + dh * P
-                        nc.tensor.matmul(
-                            out=bank[:, m * 64 : (m + 1) * 64], lhsT=xq[q][:, first : first + P], rhs=pick[:],
-                            start=(jl == 0), stop=(jl == 1),
-                        )
-                q_banks[(q, dh)] = bank
-
-        def pick_out(q):
-            for dh in range(2):
-                nc.scalar.copy(
-                    out=mean_t[:, dh * 1024 : (dh + 1) * 1024].rearrange("d (k a m x) -> d a k m x", k=4, a=2, m=8)[:, q],
-                    in_=q_banks[(q, dh)][:].rearrange("d (m k x) -> d k m x", k=4, x=16),
-                )
-
-        m_banks = {}
-
-        def mean_turn(first_bank):
-            words = mean_t[:].bitcast(F32)
-            for half in range(2):
-                bank = bank_tile(first_bank + half)
-                for dh in range(2):
-                    for u in range(2):
-                        first = dh * 512 + (2 * half + u) * P
-                        nc.tensor.transpose(
-                            bank[:, (2 * dh + u) * P : (2 * dh + u + 1) * P], words[:, first : first + P], ident[:]
-                        )
-                m_banks[half] = bank
-
-        def mean_turn_out():
-            for half in range(2):
-                nc.scalar.copy(
-                    out=mean_grp[1][:].bitcast(F32)[:, half * 512 : (half + 1) * 512].rearrange(
-                        "p (a d u) -> p a d u", a=2, u=2
-                    ),
-                    in_=m_banks[half][:].rearrange("p (a u d) -> p a d u", a=2, u=2),
-                )
-
         def mean_quantize(g):
             quantize(mean_code[g][:], mean_scale[g][:], mean_grp[g][:], E4M3)
 
         tok_grp = {}
 
-        def tok_interleave(g, h, engine):
-            grp = sb.tile([P, 2048], BF16, name="tok_grp", tag="tok_grp", bufs=4, align_bytes=64)
+        def tok_interleave(g, h, engine, lo=0, hi=2):
+            if lo == 0:
+                tok_grp[(g, h)] = sb.tile([P, 2048], BF16, name="tok_grp", tag="tok_grp", bufs=4, align_bytes=64)
             move(
                 engine,
-                out=grp[:].rearrange("p (u c i t) -> p u c t i", u=2, i=4, t=4),
-                in_=dz[:].rearrange("p (g u t h c i) -> p g h u c t i", t=4, u=2, g=2, h=2, i=4)[:, g, h],
+                out=tok_grp[(g, h)][:].rearrange("p (u c i t) -> p u c t i", u=2, i=4, t=4)[:, lo:hi],
+                in_=dz[:].rearrange("p (g u t h c i) -> p g h u c t i", t=4, u=2, g=2, h=2, i=4)[:, g, h, lo:hi],
             )
-            tok_grp[(g, h)] = grp
 
         def tok_quantize(g, h):
             quantize(tok_code[g][h][:], tok_scale[g][h][:], tok_grp[(g, h)][:], E5M2)
@@ -348,23 +294,30 @@ def tile_ferminetoneelectronlayer_pa_v_kernel(
         w_banks = {}
 
         def dw_pass(m, h, g):
-            if g == 0:
+            opens = g == h
+            if opens:
                 w_banks[(m, h)] = bank_tile(2 * m + h)
             cols = slice(m * P, (m + 1) * P)
             nc.tensor.matmul_mx(
                 out=w_banks[(m, h)][:], lhsT=mean_code[g][:, cols].bitcast(E4M3), lhsT_scale=mean_scale[g][:, cols],
-                rhs=tok_code[g][h][:].bitcast(E5M2), rhs_scale=tok_scale[g][h][:], start=(g == 0), stop=(g == 1),
+                rhs=tok_code[g][h][:].bitcast(E5M2), rhs_scale=tok_scale[g][h][:], start=opens, stop=not opens,
             )
 
         dw = {}
 
         def dw_out(m, h, engine):
-            if h == 0:
-                dw[m] = keep("dw%d" % m, FEATS, F32, tag="z%d" % m)
+            if m % 2 == 0:
+                dw[(m // 2, h)] = keep("dw%d%d" % (m // 2, h), FEATS, F32, tag="z%d" % (m + h))
             scaled_out(
                 engine,
-                out=dw[m][:, h * 512 : (h + 1) * 512].rearrange("m (w u e) -> m w u e", u=2, e=2),
+                out=dw[(m // 2, h)][:, (m % 2) * 512 : (m % 2 + 1) * 512].rearrange("m (w u e) -> m w u e", u=2, e=2),
                 in_=w_banks[(m, h)][:].rearrange("m (u w e) -> m w u e", u=2, e=2),
+            )
+
+        def dw_store(pair, h):
+            nc.sync.dma_start(
+                out=out_1[2 * pair * P : 2 * (pair + 1) * P, h * 512 : (h + 1) * 512].rearrange("(a p) f -> p a f", a=2),
+                in_=dw[(pair, h)][:].rearrange("p (a f) -> p a f", a=2),
             )
 
         tanh_squared(0, 0, 0, 1)
@@ -398,53 +351,56 @@ def tile_ferminetoneelectronlayer_pa_v_kernel(
         dz_turn(3, 0)
         d_all_out(0, "scalar", 2)
         dx_stores(0)
-        sum_matmul(0, 3, 4)
         make_dz(1, 1, 0)
         make_dz(1, 1, 1)
         dz_turn(2, 1)
         dz_turn(3, 1)
         d_all_out(1, "scalar", 2)
         dx_stores(1)
-        pick_matmul(0, 6)
         feat_out(2, "scalar")
         feat_out(3, "scalar")
-        sum_out(0, 3)
         sum_pairs(0, 0, 256)
-        sum_pairs(0, 1, 128)
         feat_quantize(2)
         d_all_matmul(2, 0)
-        pick_matmul(1, 4)
         sum_finish(0, 0, 256)
         feat_quantize(3)
         d_all_matmul(3, 2)
-        tok_interleave(0, 0, "vector")
-        pick_out(0)
+        for m in range(1, 4):
+            sum_matmul(1, m, 3 + m)
+        tok_interleave(0, 0, "scalar", 0, 1)
         d_all_out(2, "scalar", 2)
         dx_stores(2)
-        pick_out(1)
-        mean_turn(6)
+        tok_interleave(0, 0, "scalar", 1, 2)
         d_all_out(3, "scalar", 2)
         dx_stores(3)
-        mean_turn_out()
+        for m in range(1, 4):
+            sum_out(1, m)
         tok_interleave(1, 1, "scalar")
-        sum_finish(0, 1, 128)
+        sum_pairs(0, 1, 256)
+        sum_pairs(1, 0, 128)
+        sum_finish(0, 1, 256)
+        sum_finish(1, 0, 128)
+        sum_interleave(0, 512)
+        sum_interleave(1, 128)
         tok_quantize(0, 0)
-        sum_interleave(0, 384)
-        tok_interleave(0, 1, "vector")
         mean_quantize(0)
         for m in range(4):
             dw_pass(m, 0, 0)
         tok_interleave(1, 0, "vector")
-        tok_quantize(0, 1)
-        for m in range(4):
-            dw_pass(m, 1, 0)
         mean_quantize(1)
         tok_quantize(1, 0)
         for m in range(4):
             dw_pass(m, 0, 1)
+            dw_out(m, 0, "scalar")
+            if m % 2 == 1:
+                dw_store(m // 2, 0)
         tok_quantize(1, 1)
         for m in range(4):
-            dw_out(m, 0, "scalar")
             dw_pass(m, 1, 1)
-            dw_out(m, 1, "vector" if m < 3 else "scalar")
-            nc.sync.dma_start(out=out_1[m * P : (m + 1) * P, :], in_=dw[m][:])
+        tok_interleave(0, 1, "vector")
+        tok_quantize(0, 1)
+        for m in range(4):
+            dw_pass(m, 1, 0)
+            dw_out(m, 1, "vector" if m % 2 == 0 else "scalar")
+            if m % 2 == 1:
+                dw_store(m // 2, 1)

from contextlib import ExitStack

import concourse.mybir as mybir
from concourse.masks import make_identity

F32 = mybir.dt.float32
BF16 = mybir.dt.bfloat16
U32 = mybir.dt.uint32
U8 = mybir.dt.uint8
E4M3 = mybir.dt.float8_e4m3fn_x4
E5M2 = mybir.dt.float8_e5m2_x4
ACT = mybir.ActivationFunctionType
ALU = mybir.AluOpType

P = 128
TOKENS, FEATS, PAIR, COLS = 1024, 1024, 256, 512
FLOPS = 2 * 2 * TOKENS * FEATS * COLS
BYTES = 2 * 8 * TOKENS * PAIR + 2 * COLS * FEATS + 6 * TOKENS * FEATS + 4 * 8 * TOKENS * PAIR + 4 * COLS * FEATS


def tile_ferminetoneelectronlayer_pa_v_kernel(
    tc, in_1e, in_2e, W_unmixed, b_unmixed, W_mixed, W_2e, z, grad_out, out_0, out_1
):
    nc = tc.nc
    z_hbm = z.rearrange("b i f -> (b i) f").rearrange("(g p a j) f -> a g p (j f)", g=2, a=2, j=2)
    g_hbm = grad_out.rearrange("b i f -> (b i) f").rearrange("(g p j) f -> g p (j f)", g=2, j=4)
    w_hbm = W_2e.rearrange("(p r) f -> p (r f)", p=P)
    dx_hbm = out_0.rearrange("b i j d -> b (i j d)")

    with ExitStack() as ctx:
        sb = ctx.enter_context(tc.tile_pool(name="sb", bufs=1))
        ps = ctx.enter_context(tc.psum_pool(name="ps", bufs=1))
        ctx.enter_context(tc.manual_schedule())

        def keep(name, cols, dtype, tag=None):
            return sb.tile([P, cols], dtype, name=name, tag=tag or name, align_bytes=64)

        zt = [keep("z%d" % j, 2 * FEATS, F32) for j in range(4)]
        g_early = [keep("g_early%d" % g, 2 * FEATS, BF16) for g in range(2)]
        g_late = keep("g_late", 4 * FEATS, BF16)
        gt = [g_early[0][:], g_early[1][:], g_late[:, 0 : 2 * FEATS], g_late[:, 2 * FEATS :]]
        wt = keep("w", 4 * FEATS, BF16)
        xt = [keep("x%d" % g, 32 * PAIR, BF16) for g in range(2)]
        ident = keep("ident", P, F32)
        ident_bf = keep("ident_bf", P, BF16)
        dz = keep("dz", 8 * FEATS, BF16)
        w_grp = [keep("w_grp%d" % h, 2048, BF16) for h in range(2)]
        w_code = [keep("w_code%d" % h, 512, U32) for h in range(2)]
        w_scale = [keep("w_scale%d" % h, 512, U8) for h in range(2)]
        mean_grp = [keep("mean_grp%d" % g, 2048, BF16) for g in range(2)]
        mean_code = [keep("mean_code%d" % g, 512, U32) for g in range(2)]
        mean_scale = [keep("mean_scale%d" % g, 512, U8) for g in range(2)]
        tok_code = [[keep("tok_code%d%d" % (g, h), 512, U32) for h in range(2)] for g in range(2)]
        tok_scale = [[keep("tok_scale%d%d" % (g, h), 512, U8) for h in range(2)] for g in range(2)]
        stage = keep("stage", 8 * 1024, F32)
        sums = [keep("sums%d" % g, 2048, BF16) for g in range(2)]

        def load_z(a, g, lo, hi):
            nc.sync.dma_start(out=zt[2 * a + g][:, lo * FEATS : hi * FEATS], in_=z_hbm[a, g, :, lo * FEATS : hi * FEATS])

        def load_g(g, lo, hi):
            nc.sync.dma_start(out=gt[g][:, lo * FEATS : hi * FEATS], in_=g_hbm[g, :, lo * FEATS : hi * FEATS])

        def load_g_late():
            nc.sync.dma_start(
                out=g_late[:].rearrange("p (g x) -> p g x", g=2),
                in_=g_hbm.rearrange("g p x -> p g x")[:, :, 2 * FEATS :],
            )

        def load_x(g):
            walkers = in_2e[64 * g : 64 * g + 64]
            nc.sync.dma_start(out=xt[g][0:P:2, :], in_=walkers[:, 0:4].rearrange("b i j d -> b (i j d)"))
            for half in range(2):
                c = 1 - half
                nc.sync.dma_start(
                    out=xt[g][1:P:2, :].rearrange("p (i a x) -> p a i x", i=4, a=2)[:, half],
                    in_=walkers[:, 4:8, 4 * c : 4 * c + 4].rearrange("b i j d -> b i (j d)"),
                )

        def load_w(lo, hi):
            nc.sync.dma_start(out=wt[:, lo * 2048 : hi * 2048], in_=w_hbm[:, lo * 2048 : hi * 2048])

        load_z(0, 0, 0, 1)
        load_w(0, 1)
        load_z(0, 0, 1, 2)
        load_z(0, 1, 0, 2)
        load_g(0, 0, 2)
        load_w(1, 2)
        load_z(1, 0, 0, 2)
        load_g(1, 0, 2)
        load_z(1, 1, 0, 2)
        load_g_late()
        load_x(0)
        load_x(1)

        make_identity(nc, ident[:])
        make_identity(nc, ident_bf[:])

        def bank_tile(n):
            return ps.tile([P, 512], F32, name="bank%d" % n, tag="bank%d" % n)

        def quantize(code, scale, src, fmt):
            nc.vector.quantize_mx(out=code.bitcast(fmt), scales=scale, in_=src)

        def tanh_squared(a, g, lo=0, hi=2, engine="scalar"):
            part = zt[2 * a + g][:, lo * FEATS : hi * FEATS]
            nc.scalar.activation(out=part, in_=part, func=ACT.Tanh)
            if engine == "scalar":
                nc.scalar.activation(out=part, in_=part, func=ACT.Square)
            else:
                nc.vector.tensor_tensor(out=part, in0=part, in1=part, op=ALU.mult)

        def w_turn(h, rp):
            words = wt[:].bitcast(F32)
            bank = bank_tile(4 + 2 * rp + h)
            for r in range(2):
                for u in range(2):
                    first = (2 * rp + r) * 512 + h * 256
                    nc.tensor.transpose(
                        bank[:, (2 * r + u) * P : (2 * r + u + 1) * P], words[:, first + u : first + 256 : 2], ident[:]
                    )
            nc.vector.tensor_copy(
                out=w_grp[h][:].bitcast(F32).rearrange("q (p a r u) -> q a p r u", a=2, r=2, u=2)[:, rp],
                in_=bank[:].rearrange("q (r u p) -> q p r u", r=2, u=2),
            )

        def w_quantize(h):
            quantize(w_code[h][:], w_scale[h][:], w_grp[h][:], E4M3)

        def move(engine, out, in_):
            if engine == "scalar":
                nc.scalar.copy(out=out, in_=in_)
            else:
                nc.vector.tensor_copy(out=out, in_=in_)

        def make_dz(a, g, u, lo=0, hi=2):
            first = g * 4096 + u * 2048 + a * 1024
            nc.vector.scalar_tensor_tensor(
                out=dz[:, first + lo * 512 : first + hi * 512].rearrange("p (n e) -> p n e", e=2),
                in0=zt[2 * a + g][:, lo * FEATS : hi * FEATS].rearrange("p (n u e) -> p u n e", u=2, e=2)[:, u],
                scalar=1.0,
                in1=gt[2 * a + g][:, lo * FEATS : hi * FEATS].rearrange("p (n u e) -> p u n e", u=2, e=2)[:, u],
                op0=ALU.subtract,
                op1=ALU.mult,
            )

        feat = {}

        f_banks = {}

        def dz_turn(j, g):
            words = dz[:].bitcast(F32)
            if g == 0:
                f_banks[j] = [bank_tile(2 * (j % 2) + h) for h in range(2)]
            for u in range(2):
                for h in range(2):
                    first = g * 2048 + u * 1024 + j * 256 + h * P
                    nc.tensor.transpose(
                        f_banks[j][h][:, (2 * g + u) * P : (2 * g + u + 1) * P], words[:, first : first + P], ident[:]
                    )

        def feat_out(j, engine):
            banks = f_banks[j]
            grp = sb.tile([P, 2048], BF16, name="feat_grp", tag="feat_grp", bufs=2, align_bytes=64)
            code = sb.tile([P, 512], U32, name="feat_code", tag="feat_code", bufs=2, align_bytes=64)
            scale = sb.tile([P, 512], U8, name="feat_scale", tag="feat_scale", bufs=2, align_bytes=64)
            for h in range(2):
                move(
                    engine,
                    out=grp[:].bitcast(F32)[:, h * 512 : (h + 1) * 512].rearrange(
                        "q (s g b u) -> q s g b u", s=2, g=2, u=2
                    ),
                    in_=banks[h][:].rearrange("q (g u b s) -> q s g b u", g=2, u=2, s=2),
                )
            feat[j] = (code, scale, grp)

        def feat_quantize(j):
            code, scale, grp = feat[j]
            for h in range(2):
                quantize(
                    code[:, h * 256 : (h + 1) * 256], scale[:, h * 256 : (h + 1) * 256],
                    grp[:, h * 1024 : (h + 1) * 1024], E5M2,
                )

        d_banks = {}

        def d_all_matmul(j, first_bank):
            code, scale, grp = feat[j]
            for s in range(2):
                bank = bank_tile(first_bank + s)
                for h in range(2):
                    cols = slice((2 * h + s) * P, (2 * h + s + 1) * P)
                    nc.tensor.matmul_mx(
                        out=bank[:], lhsT=code[:, cols].bitcast(E5M2), lhsT_scale=scale[:, cols],
                        rhs=w_code[h][:].bitcast(E4M3), rhs_scale=w_scale[h][:], start=(h == 0), stop=(h == 1),
                    )
                d_banks[(j, s)] = bank

        def scaled_out(engine, out, in_):
            if engine == "scalar":
                nc.scalar.activation(out=out, in_=in_, func=ACT.Copy, scale=-0.25)
            else:
                nc.vector.tensor_scalar(out=out, in0=in_, scalar1=-0.25, scalar2=None, op0=ALU.mult)

        def d_all_out(j, engine, reps):
            for s in range(2):
                i = 4 * s + j
                dst = stage[:, i * 1024 : (i + 1) * 1024].rearrange("b (c r d) -> b c r d", c=2, r=2)
                src = d_banks[(j, s)][:].rearrange("b (a d) -> b a d", a=2)
                if s == 0:
                    scaled_out(engine, dst[:, :, 0:reps], src.unsqueeze(2).to_broadcast([P, 2, reps, PAIR]))
                else:
                    for c in range(2):
                        scaled_out(
                            engine, dst[:, c, 0:reps], src[:, 1 - c].unsqueeze(1).to_broadcast([P, reps, PAIR])
                        )

        def d_all_repeat(j):
            both = stage[:].rearrange("b (s j c r d) -> b j r s c d", s=2, j=4, c=2, r=2)[:, j]
            nc.vector.tensor_copy(out=both[:, 1], in_=both[:, 0])

        def dx_store(first, last, shift):
            src = stage[:, shift : shift + 7 * 1024 + (1024 if shift == 0 else 0)].rearrange("b (i x) -> b i x", x=1024)
            dst = dx_hbm[:, 2 * shift : 2 * shift + (8 if shift == 0 else 7) * 2048].rearrange("b (i x) -> b i x", x=2048)
            step = max(last - first, 1)
            nc.sync.dma_start(out=dst[:, first : last + 1 : step, 512:1536], in_=src[:, first : last + 1 : step])

        def dx_stores(j):
            if j == 0:
                nc.sync.dma_start(out=dx_hbm[:, 0:512], in_=stage[:, 0:512])
            dx_store(j, 4 + j, 0)
            if j > 0:
                dx_store(j - 1, 3 + j, 512)
            if j == 3:
                dx_store(3, 3, 512)
                nc.sync.dma_start(out=dx_hbm[:, 16384 - 512 :], in_=stage[:, 8192 - 512 :])

        s_banks = {}

        def sum_matmul(g, m, bank_no):
            half, dh = divmod(m, 2)
            bank = bank_tile(bank_no)
            rows = xt[g][:].rearrange("p (i a j h d) -> p a h j i d", i=4, a=2, j=4, h=2)[:, half, dh]
            for jj in range(4):
                nc.tensor.matmul(
                    out=bank[:].rearrange("p (i d) -> p i d", i=4), lhsT=ident_bf[:], rhs=rows[:, jj],
                    start=(jj == 0), stop=(jj == 3),
                )
            s_banks[(g, m)] = bank

        def sum_out(g, m):
            nc.scalar.copy(
                out=mean_grp[g][:, m * 512 : (m + 1) * 512].rearrange("p (d i) -> p d i", i=4),
                in_=s_banks[(g, m)][:].rearrange("p (i d) -> p d i", i=4),
            )

        pairs = {}

        def sum_pairs(g, half, width):
            tmp = sb.tile([P, 2048], F32, name="pairs", tag="pairs", bufs=2, align_bytes=64)
            rows = xt[g][:].rearrange("p (i a k j d) -> p a k i j d", i=4, a=2, k=2, j=2)[:, half]
            view = tmp[:].rearrange("p (i j d) -> p i j d", i=4, j=2)[:, :, :, 0:width]
            nc.vector.tensor_tensor(out=view, in0=rows[:, 0, :, :, 0:width], in1=rows[:, 1, :, :, 0:width], op=ALU.add)
            pairs[(g, half)] = view

        def sum_finish(g, half, width):
            view = pairs[(g, half)]
            dst = sums[g][:].rearrange("p (i a d) -> p a i d", i=4, a=2)[:, half, :, 0:width]
            nc.vector.tensor_tensor(out=dst, in0=view[:, :, 0], in1=view[:, :, 1], op=ALU.add)

        def sum_interleave(g, width):
            nc.vector.tensor_copy(
                out=mean_grp[g][:, 0 : 4 * width].rearrange("p (c i t) -> p c t i", i=4, t=4),
                in_=sums[g][:].rearrange("p (t n) -> p t n", t=4)[:, :, 0:width].rearrange("p t (c i) -> p c t i", i=4),
            )

        def mean_quantize(g):
            quantize(mean_code[g][:], mean_scale[g][:], mean_grp[g][:], E4M3)

        tok_grp = {}

        def tok_interleave(g, h, engine, lo=0, hi=2):
            if lo == 0:
                tok_grp[(g, h)] = sb.tile([P, 2048], BF16, name="tok_grp", tag="tok_grp", bufs=4, align_bytes=64)
            move(
                engine,
                out=tok_grp[(g, h)][:].rearrange("p (u c i t) -> p u c t i", u=2, i=4, t=4)[:, lo:hi],
                in_=dz[:].rearrange("p (g u t h c i) -> p g h u c t i", t=4, u=2, g=2, h=2, i=4)[:, g, h, lo:hi],
            )

        def tok_quantize(g, h):
            quantize(tok_code[g][h][:], tok_scale[g][h][:], tok_grp[(g, h)][:], E5M2)

        w_banks = {}

        def dw_pass(m, h, g):
            opens = g == h
            if opens:
                w_banks[(m, h)] = bank_tile(2 * m + h)
            cols = slice(m * P, (m + 1) * P)
            nc.tensor.matmul_mx(
                out=w_banks[(m, h)][:], lhsT=mean_code[g][:, cols].bitcast(E4M3), lhsT_scale=mean_scale[g][:, cols],
                rhs=tok_code[g][h][:].bitcast(E5M2), rhs_scale=tok_scale[g][h][:], start=opens, stop=not opens,
            )

        dw = {}

        def dw_out(m, h, engine):
            if m % 2 == 0:
                dw[(m // 2, h)] = keep("dw%d%d" % (m // 2, h), FEATS, F32, tag="z%d" % (m + h))
            scaled_out(
                engine,
                out=dw[(m // 2, h)][:, (m % 2) * 512 : (m % 2 + 1) * 512].rearrange("m (w u e) -> m w u e", u=2, e=2),
                in_=w_banks[(m, h)][:].rearrange("m (u w e) -> m w u e", u=2, e=2),
            )

        def dw_store(pair, h):
            nc.sync.dma_start(
                out=out_1[2 * pair * P : 2 * (pair + 1) * P, h * 512 : (h + 1) * 512].rearrange("(a p) f -> p a f", a=2),
                in_=dw[(pair, h)][:].rearrange("p (a f) -> p a f", a=2),
            )

        tanh_squared(0, 0, 0, 1)
        w_turn(0, 0)
        w_turn(1, 0)
        tanh_squared(0, 0, 1, 2)
        make_dz(0, 0, 0)
        make_dz(0, 0, 1)
        tanh_squared(0, 1)
        w_turn(0, 1)
        w_turn(1, 1)
        dz_turn(0, 0)
        dz_turn(1, 0)
        w_quantize(0)
        tanh_squared(1, 0)
        make_dz(0, 1, 0)
        make_dz(0, 1, 1)
        w_quantize(1)
        dz_turn(0, 1)
        dz_turn(1, 1)
        feat_out(0, "vector")
        feat_out(1, "vector")
        feat_quantize(0)
        d_all_matmul(0, 4)
        tanh_squared(1, 1)
        make_dz(1, 0, 0)
        feat_quantize(1)
        d_all_matmul(1, 6)
        make_dz(1, 0, 1)
        dz_turn(2, 0)
        dz_turn(3, 0)
        d_all_out(0, "scalar", 2)
        dx_stores(0)
        make_dz(1, 1, 0)
        make_dz(1, 1, 1)
        dz_turn(2, 1)
        dz_turn(3, 1)
        d_all_out(1, "scalar", 2)
        dx_stores(1)
        feat_out(2, "scalar")
        feat_out(3, "scalar")
        sum_pairs(0, 0, 256)
        feat_quantize(2)
        d_all_matmul(2, 0)
        sum_finish(0, 0, 256)
        feat_quantize(3)
        d_all_matmul(3, 2)
        for m in range(1, 4):
            sum_matmul(1, m, 3 + m)
        tok_interleave(0, 0, "scalar", 0, 1)
        d_all_out(2, "scalar", 2)
        dx_stores(2)
        tok_interleave(0, 0, "scalar", 1, 2)
        d_all_out(3, "scalar", 2)
        dx_stores(3)
        for m in range(1, 4):
            sum_out(1, m)
        tok_interleave(1, 1, "scalar")
        sum_pairs(0, 1, 256)
        sum_pairs(1, 0, 128)
        sum_finish(0, 1, 256)
        sum_finish(1, 0, 128)
        sum_interleave(0, 512)
        sum_interleave(1, 128)
        tok_quantize(0, 0)
        mean_quantize(0)
        for m in range(4):
            dw_pass(m, 0, 0)
        tok_interleave(1, 0, "vector")
        mean_quantize(1)
        tok_quantize(1, 0)
        for m in range(4):
            dw_pass(m, 0, 1)
            dw_out(m, 0, "scalar")
            if m % 2 == 1:
                dw_store(m // 2, 0)
        tok_quantize(1, 1)
        for m in range(4):
            dw_pass(m, 1, 1)
        tok_interleave(0, 1, "vector")
        tok_quantize(0, 1)
        for m in range(4):
            dw_pass(m, 1, 0)
            dw_out(m, 1, "vector" if m % 2 == 0 else "scalar")
            if m % 2 == 1:
                dw_store(m // 2, 1)
